import numpy as np
import ml_dtypes

BF16 = ml_dtypes.bfloat16


def bf(x):
    return np.asarray(x, np.float32).astype(BF16)


def f32(x):
    return np.asarray(x, np.float32)


def f64(x):
    return np.asarray(x).astype(np.float64)


def striped(idx):
    return np.tile(idx.reshape(-1, 16).T, (8, 1))


C, S, N = 768, 512, 1024
EPS = 1e-5


def setup_inputs():
    return {"tok_emb": f32(np.random.standard_normal((C, S))), "pos_emb": f32(np.random.standard_normal((C, N))), "type_emb": f32(0.5 * np.random.standard_normal((C, 1))), "lnf_w": f32(1.0 + 0.1 * np.random.standard_normal((C, 1))), "lnf_b": f32(0.1 * np.random.standard_normal((C, 1))), "offs": striped(np.random.permutation(np.tile(np.arange(S), 2))[:N])}


def reference(tok_emb, pos_emb, type_emb, lnf_w, lnf_b, offs):
    idx = offs[:16].T.reshape(-1)
    e = f64(tok_emb)[:, idx] + f64(pos_emb) + f64(type_emb)
    mean = e.mean(axis=0, keepdims=True)
    var = ((e - mean) ** 2).mean(axis=0, keepdims=True)
    return (e - mean) / np.sqrt(var + EPS) * f64(lnf_w) + f64(lnf_b)

@@ -1,0 +1,104 @@
+import concourse.mybir as mybir
+from concourse.masks import make_identity
+
+F32, BF16, U16 = mybir.dt.float32, mybir.dt.bfloat16, mybir.dt.uint16
+ADD, SUBTRACT, MULT = mybir.AluOpType.add, mybir.AluOpType.subtract, mybir.AluOpType.mult
+FUNC = mybir.ActivationFunctionType
+
+P = 128
+C, S, N = 768, 512, 1024
+EPS = 1e-5
+BLOCKS = C // P
+PIECE = 512
+PIECES = N // PIECE
+LIST_COLUMNS = PIECE // 16
+
+
+def tile_gpt_kernel(tc, tok_emb, pos_emb, type_emb, lnf_w, lnf_b, offs, out):
+    nc = tc.nc
+    with (
+        tc.tile_pool(name="held", bufs=1) as held,
+        tc.tile_pool(name="ring", bufs=4) as ring,
+        tc.psum_pool(name="psum", bufs=1) as psum,
+    ):
+        offsets = held.tile([P, N // 16], U16, name="offsets")
+        nc.sync.dma_start(offsets[:], offs)
+
+        vector_rows = held.tile([P, P], F32, name="vector_rows")
+        nc.vector.memset(vector_rows[:], 0.0)
+        for k, vector in enumerate((type_emb, lnf_w, lnf_b)):
+            nc.sync.dma_start(
+                vector_rows[k * BLOCKS : (k + 1) * BLOCKS, :], vector.rearrange("(b p) o -> b (p o)", p=P)
+            )
+
+        tok = [held.tile([P, S], F32, name=f"tok{b}") for b in range(BLOCKS)]
+        pos = [[held.tile([P, PIECE], F32, name=f"pos{p}_{b}") for b in range(BLOCKS)] for p in range(PIECES)]
+        for p in range(PIECES):
+            for b in range(BLOCKS):
+                if p == 0:
+                    nc.sync.dma_start(tok[b][:], tok_emb[b * P : (b + 1) * P, :])
+                nc.sync.dma_start(pos[p][b][:], pos_emb[b * P : (b + 1) * P, p * PIECE : (p + 1) * PIECE])
+
+        average = held.tile([P, P], F32, name="average")
+        nc.vector.memset(average[:], 1.0 / C)
+        ones = held.tile([P, P], BF16, name="ones")
+        nc.vector.memset(ones[:], 1.0)
+        eps = held.tile([P, 1], F32, name="eps")
+        nc.vector.memset(eps[:], EPS)
+        identity = held.tile([P, P], F32, name="identity")
+        make_identity(nc, identity[:])
+
+        summed = [[held.tile([P, PIECE], F32, name=f"summed{p}_{b}") for b in range(BLOCKS)] for p in range(PIECES)]
+        centred = [[held.tile([P, PIECE], F32, name=f"centred{p}_{b}") for b in range(BLOCKS)] for p in range(PIECES)]
+        mean = [psum.tile([P, PIECE], F32, name=f"mean{p}") for p in range(PIECES)]
+        square_sum = [psum.tile([P, PIECE], F32, name=f"square_sum{p}") for p in range(PIECES)]
+        rstd = [held.tile([P, PIECE], F32, name=f"rstd{p}") for p in range(PIECES)]
+
+        def gather(p):
+            piece_offsets = offsets[:, p * LIST_COLUMNS : (p + 1) * LIST_COLUMNS]
+            for b in range(BLOCKS):
+                nc.vector.tensor_tensor(summed[p][b][:], tok[b][:].indirect(piece_offsets), pos[p][b][:], ADD)
+                nc.tensor.matmul(mean[p][:], average[:], summed[p][b][:], start=(b == 0), stop=(b == BLOCKS - 1))
+
+        def centre(p):
+            for b in range(BLOCKS):
+                nc.vector.scalar_tensor_tensor(
+                    centred[p][b][:], summed[p][b][:], type_centred[:, b : b + 1], mean[p][:], ADD, SUBTRACT
+                )
+                squares = ring.tile([P, PIECE], BF16, name="squares")
+                nc.scalar.activation(squares[:], centred[p][b][:], FUNC.Square)
+                nc.tensor.matmul(square_sum[p][:], ones[:], squares[:], start=(b == 0), stop=(b == BLOCKS - 1))
+            nc.scalar.activation(rstd[p][:], square_sum[p][:], FUNC.Abs_reciprocal_sqrt, bias=eps[:], scale=1.0 / C)
+
+        def scale(p):
+            for b in range(BLOCKS):
+                normed = ring.tile([P, PIECE], F32, name="normed")
+                nc.vector.tensor_tensor(normed[:], centred[p][b][:], rstd[p][:], MULT)
+                result = ring.tile([P, PIECE], F32, name="result")
+                nc.scalar.activation(
+                    result[:], normed[:], FUNC.Identity, bias=lnf_b_columns[:, b : b + 1], scale=lnf_w_columns[:, b : b + 1]
+                )
+                nc.sync.dma_start(out[b * P : (b + 1) * P, p * PIECE : (p + 1) * PIECE], result[:])
+
+        gather(0)
+
+        columns_psum = psum.tile([P, P], F32, name="columns_psum")
+        nc.tensor.transpose(columns_psum[:], vector_rows[:], identity[:])
+        columns = held.tile([P, 3 * BLOCKS], F32, name="columns")
+        nc.vector.tensor_copy(columns[:], columns_psum[:, 0 : 3 * BLOCKS])
+        type_columns = columns[:, 0:BLOCKS]
+        lnf_w_columns = columns[:, BLOCKS : 2 * BLOCKS]
+        lnf_b_columns = columns[:, 2 * BLOCKS : 3 * BLOCKS]
+
+        type_block_means = psum.tile([P, BLOCKS], F32, name="type_block_means")
+        nc.tensor.matmul(type_block_means[:], average[:], type_columns, start=True, stop=True)
+        type_mean = held.tile([P, 1], F32, name="type_mean")
+        nc.vector.reduce_sum(type_mean[:], type_block_means[:], axis=mybir.AxisListType.X)
+        type_centred = held.tile([P, BLOCKS], F32, name="type_centred")
+        nc.vector.tensor_scalar(type_centred[:], type_columns, type_mean[:], None, SUBTRACT)
+
+        centre(0)
+        gather(1)
+        centre(1)
+        scale(0)
+        scale(1)

@@ -27,7 +27,7 @@ def tile_gpt_kernel(tc, tok_emb, pos_emb, type_emb, lnf_w, lnf_b, offs, out):
         vector_rows = held.tile([P, P], F32, name="vector_rows")
         nc.vector.memset(vector_rows[:], 0.0)
         for k, vector in enumerate((type_emb, lnf_w, lnf_b)):
-            nc.sync.dma_start(
+            nc.scalar.dma_start(
                 vector_rows[k * BLOCKS : (k + 1) * BLOCKS, :], vector.rearrange("(b p) o -> b (p o)", p=P)
             )
 
@@ -53,6 +53,8 @@ def tile_gpt_kernel(tc, tok_emb, pos_emb, type_emb, lnf_w, lnf_b, offs, out):
         mean = [psum.tile([P, PIECE], F32, name=f"mean{p}") for p in range(PIECES)]
         square_sum = [psum.tile([P, PIECE], F32, name=f"square_sum{p}") for p in range(PIECES)]
         rstd = [held.tile([P, PIECE], F32, name=f"rstd{p}") for p in range(PIECES)]
+        normed = [[held.tile([P, PIECE], F32, name=f"normed{p}_{b}") for b in range(BLOCKS)] for p in range(PIECES)]
+        result = [[held.tile([P, PIECE], F32, name=f"result{p}_{b}") for b in range(BLOCKS)] for p in range(PIECES)]
 
         def gather(p):
             piece_offsets = offsets[:, p * LIST_COLUMNS : (p + 1) * LIST_COLUMNS]
@@ -72,15 +74,15 @@ def tile_gpt_kernel(tc, tok_emb, pos_emb, type_emb, lnf_w, lnf_b, offs, out):
 
         def scale(p):
             for b in range(BLOCKS):
-                normed = ring.tile([P, PIECE], F32, name="normed")
-                nc.vector.tensor_tensor(normed[:], centred[p][b][:], rstd[p][:], MULT)
-                result = ring.tile([P, PIECE], F32, name="result")
+                nc.vector.tensor_tensor(normed[p][b][:], centred[p][b][:], rstd[p][:], MULT)
                 nc.scalar.activation(
-                    result[:], normed[:], FUNC.Identity, bias=lnf_b_columns[:, b : b + 1], scale=lnf_w_columns[:, b : b + 1]
+                    result[p][b][:],
+                    normed[p][b][:],
+                    FUNC.Identity,
+                    bias=lnf_b_columns[:, b : b + 1],
+                    scale=lnf_w_columns[:, b : b + 1],
                 )
-                nc.sync.dma_start(out[b * P : (b + 1) * P, p * PIECE : (p + 1) * PIECE], result[:])
-
-        gather(0)
+                nc.sync.dma_start(out[b * P : (b + 1) * P, p * PIECE : (p + 1) * PIECE], result[p][b][:])
 
         columns_psum = psum.tile([P, P], F32, name="columns_psum")
         nc.tensor.transpose(columns_psum[:], vector_rows[:], identity[:])
@@ -97,6 +99,7 @@ def tile_gpt_kernel(tc, tok_emb, pos_emb, type_emb, lnf_w, lnf_b, offs, out):
         type_centred = held.tile([P, BLOCKS], F32, name="type_centred")
         nc.vector.tensor_scalar(type_centred[:], type_columns, type_mean[:], None, SUBTRACT)
 
+        gather(0)
         centre(0)
         gather(1)
         centre(1)

@@ -37,7 +37,7 @@ def tile_gpt_kernel(tc, tok_emb, pos_emb, type_emb, lnf_w, lnf_b, offs, out):
             for b in range(BLOCKS):
                 if p == 0:
                     nc.sync.dma_start(tok[b][:], tok_emb[b * P : (b + 1) * P, :])
-                nc.sync.dma_start(pos[p][b][:], pos_emb[b * P : (b + 1) * P, p * PIECE : (p + 1) * PIECE])
+                nc.scalar.dma_start(pos[p][b][:], pos_emb[b * P : (b + 1) * P, p * PIECE : (p + 1) * PIECE])
 
         average = held.tile([P, P], F32, name="average")
         nc.vector.memset(average[:], 1.0 / C)

@@ -18,7 +18,6 @@ def tile_gpt_kernel(tc, tok_emb, pos_emb, type_emb, lnf_w, lnf_b, offs, out):
     nc = tc.nc
     with (
         tc.tile_pool(name="held", bufs=1) as held,
-        tc.tile_pool(name="ring", bufs=4) as ring,
         tc.psum_pool(name="psum", bufs=1) as psum,
     ):
         offsets = held.tile([P, N // 16], U16, name="offsets")
@@ -37,7 +36,7 @@ def tile_gpt_kernel(tc, tok_emb, pos_emb, type_emb, lnf_w, lnf_b, offs, out):
             for b in range(BLOCKS):
                 if p == 0:
                     nc.sync.dma_start(tok[b][:], tok_emb[b * P : (b + 1) * P, :])
-                nc.scalar.dma_start(pos[p][b][:], pos_emb[b * P : (b + 1) * P, p * PIECE : (p + 1) * PIECE])
+                nc.sync.dma_start(pos[p][b][:], pos_emb[b * P : (b + 1) * P, p * PIECE : (p + 1) * PIECE])
 
         average = held.tile([P, P], F32, name="average")
         nc.vector.memset(average[:], 1.0 / C)
@@ -45,11 +44,14 @@ def tile_gpt_kernel(tc, tok_emb, pos_emb, type_emb, lnf_w, lnf_b, offs, out):
         nc.vector.memset(ones[:], 1.0)
         eps = held.tile([P, 1], F32, name="eps")
         nc.vector.memset(eps[:], EPS)
+        warm = held.tile([P, 1], F32, name="warm")
+        nc.scalar.activation(warm[:], eps[:], FUNC.Abs_reciprocal_sqrt)
         identity = held.tile([P, P], F32, name="identity")
         make_identity(nc, identity[:])
 
         summed = [[held.tile([P, PIECE], F32, name=f"summed{p}_{b}") for b in range(BLOCKS)] for p in range(PIECES)]
         centred = [[held.tile([P, PIECE], F32, name=f"centred{p}_{b}") for b in range(BLOCKS)] for p in range(PIECES)]
+        squares = [[held.tile([P, PIECE], BF16, name=f"squares{p}_{b}") for b in range(BLOCKS)] for p in range(PIECES)]
         mean = [psum.tile([P, PIECE], F32, name=f"mean{p}") for p in range(PIECES)]
         square_sum = [psum.tile([P, PIECE], F32, name=f"square_sum{p}") for p in range(PIECES)]
         rstd = [held.tile([P, PIECE], F32, name=f"rstd{p}") for p in range(PIECES)]
@@ -67,9 +69,8 @@ def tile_gpt_kernel(tc, tok_emb, pos_emb, type_emb, lnf_w, lnf_b, offs, out):
                 nc.vector.scalar_tensor_tensor(
                     centred[p][b][:], summed[p][b][:], type_centred[:, b : b + 1], mean[p][:], ADD, SUBTRACT
                 )
-                squares = ring.tile([P, PIECE], BF16, name="squares")
-                nc.scalar.activation(squares[:], centred[p][b][:], FUNC.Square)
-                nc.tensor.matmul(square_sum[p][:], ones[:], squares[:], start=(b == 0), stop=(b == BLOCKS - 1))
+                nc.scalar.activation(squares[p][b][:], centred[p][b][:], FUNC.Square)
+                nc.tensor.matmul(square_sum[p][:], ones[:], squares[p][b][:], start=(b == 0), stop=(b == BLOCKS - 1))
             nc.scalar.activation(rstd[p][:], square_sum[p][:], FUNC.Abs_reciprocal_sqrt, bias=eps[:], scale=1.0 / C)
 
         def scale(p):
@@ -100,8 +101,8 @@ def tile_gpt_kernel(tc, tok_emb, pos_emb, type_emb, lnf_w, lnf_b, offs, out):
         nc.vector.tensor_scalar(type_centred[:], type_columns, type_mean[:], None, SUBTRACT)
 
         gather(0)
-        centre(0)
         gather(1)
+        centre(0)
         centre(1)
         scale(0)
         scale(1)

@@ -85,23 +85,27 @@ def tile_gpt_kernel(tc, tok_emb, pos_emb, type_emb, lnf_w, lnf_b, offs, out):
                 )
                 nc.sync.dma_start(out[b * P : (b + 1) * P, p * PIECE : (p + 1) * PIECE], result[p][b][:])
 
+
         columns_psum = psum.tile([P, P], F32, name="columns_psum")
         nc.tensor.transpose(columns_psum[:], vector_rows[:], identity[:])
+
+        gather(0)
+
         columns = held.tile([P, 3 * BLOCKS], F32, name="columns")
         nc.vector.tensor_copy(columns[:], columns_psum[:, 0 : 3 * BLOCKS])
         type_columns = columns[:, 0:BLOCKS]
         lnf_w_columns = columns[:, BLOCKS : 2 * BLOCKS]
         lnf_b_columns = columns[:, 2 * BLOCKS : 3 * BLOCKS]
-
         type_block_means = psum.tile([P, BLOCKS], F32, name="type_block_means")
         nc.tensor.matmul(type_block_means[:], average[:], type_columns, start=True, stop=True)
+
+        gather(1)
+
         type_mean = held.tile([P, 1], F32, name="type_mean")
         nc.vector.reduce_sum(type_mean[:], type_block_means[:], axis=mybir.AxisListType.X)
         type_centred = held.tile([P, BLOCKS], F32, name="type_centred")
         nc.vector.tensor_scalar(type_centred[:], type_columns, type_mean[:], None, SUBTRACT)
 
-        gather(0)
-        gather(1)
         centre(0)
         centre(1)
         scale(0)

@@ -76,36 +76,37 @@ def tile_gpt_kernel(tc, tok_emb, pos_emb, type_emb, lnf_w, lnf_b, offs, out):
         def scale(p):
             for b in range(BLOCKS):
                 nc.vector.tensor_tensor(normed[p][b][:], centred[p][b][:], rstd[p][:], MULT)
-                nc.scalar.activation(
-                    result[p][b][:],
-                    normed[p][b][:],
-                    FUNC.Identity,
-                    bias=lnf_b_columns[:, b : b + 1],
-                    scale=lnf_w_columns[:, b : b + 1],
-                )
+                if b < BLOCKS - 1:
+                    nc.scalar.activation(
+                        result[p][b][:],
+                        normed[p][b][:],
+                        FUNC.Identity,
+                        bias=lnf_b_columns[:, b : b + 1],
+                        scale=lnf_w_columns[:, b : b + 1],
+                    )
+                else:
+                    nc.vector.tensor_scalar(
+                        result[p][b][:], normed[p][b][:], lnf_w_columns[:, b : b + 1], lnf_b_columns[:, b : b + 1], MULT, ADD
+                    )
                 nc.sync.dma_start(out[b * P : (b + 1) * P, p * PIECE : (p + 1) * PIECE], result[p][b][:])
-
 
         columns_psum = psum.tile([P, P], F32, name="columns_psum")
         nc.tensor.transpose(columns_psum[:], vector_rows[:], identity[:])
-
-        gather(0)
-
         columns = held.tile([P, 3 * BLOCKS], F32, name="columns")
         nc.vector.tensor_copy(columns[:], columns_psum[:, 0 : 3 * BLOCKS])
         type_columns = columns[:, 0:BLOCKS]
         lnf_w_columns = columns[:, BLOCKS : 2 * BLOCKS]
         lnf_b_columns = columns[:, 2 * BLOCKS : 3 * BLOCKS]
+
         type_block_means = psum.tile([P, BLOCKS], F32, name="type_block_means")
         nc.tensor.matmul(type_block_means[:], average[:], type_columns, start=True, stop=True)
-
-        gather(1)
-
         type_mean = held.tile([P, 1], F32, name="type_mean")
         nc.vector.reduce_sum(type_mean[:], type_block_means[:], axis=mybir.AxisListType.X)
         type_centred = held.tile([P, BLOCKS], F32, name="type_centred")
         nc.vector.tensor_scalar(type_centred[:], type_columns, type_mean[:], None, SUBTRACT)
 
+        gather(0)
+        gather(1)
         centre(0)
         centre(1)
         scale(0)

@@ -24,7 +24,7 @@ def tile_gpt_kernel(tc, tok_emb, pos_emb, type_emb, lnf_w, lnf_b, offs, out):
         nc.sync.dma_start(offsets[:], offs)
 
         vector_rows = held.tile([P, P], F32, name="vector_rows")
-        nc.vector.memset(vector_rows[:], 0.0)
+        nc.gpsimd.memset(vector_rows[:], 0.0)
         for k, vector in enumerate((type_emb, lnf_w, lnf_b)):
             nc.scalar.dma_start(
                 vector_rows[k * BLOCKS : (k + 1) * BLOCKS, :], vector.rearrange("(b p) o -> b (p o)", p=P)
@@ -39,11 +39,11 @@ def tile_gpt_kernel(tc, tok_emb, pos_emb, type_emb, lnf_w, lnf_b, offs, out):
                 nc.sync.dma_start(pos[p][b][:], pos_emb[b * P : (b + 1) * P, p * PIECE : (p + 1) * PIECE])
 
         average = held.tile([P, P], F32, name="average")
-        nc.vector.memset(average[:], 1.0 / C)
+        nc.gpsimd.memset(average[:], 1.0 / C)
         ones = held.tile([P, P], BF16, name="ones")
-        nc.vector.memset(ones[:], 1.0)
+        nc.gpsimd.memset(ones[:], 1.0)
         eps = held.tile([P, 1], F32, name="eps")
-        nc.vector.memset(eps[:], EPS)
+        nc.gpsimd.memset(eps[:], EPS)
         warm = held.tile([P, 1], F32, name="warm")
         nc.scalar.activation(warm[:], eps[:], FUNC.Abs_reciprocal_sqrt)
         identity = held.tile([P, P], F32, name="identity")
@@ -93,17 +93,20 @@ def tile_gpt_kernel(tc, tok_emb, pos_emb, type_emb, lnf_w, lnf_b, offs, out):
         columns_psum = psum.tile([P, P], F32, name="columns_psum")
         nc.tensor.transpose(columns_psum[:], vector_rows[:], identity[:])
         columns = held.tile([P, 3 * BLOCKS], F32, name="columns")
-        nc.vector.tensor_copy(columns[:], columns_psum[:, 0 : 3 * BLOCKS])
+        nc.scalar.copy(columns[:], columns_psum[:, 0 : 3 * BLOCKS])
         type_columns = columns[:, 0:BLOCKS]
         lnf_w_columns = columns[:, BLOCKS : 2 * BLOCKS]
         lnf_b_columns = columns[:, 2 * BLOCKS : 3 * BLOCKS]
 
         type_block_means = psum.tile([P, BLOCKS], F32, name="type_block_means")
         nc.tensor.matmul(type_block_means[:], average[:], type_columns, start=True, stop=True)
-        type_mean = held.tile([P, 1], F32, name="type_mean")
-        nc.vector.reduce_sum(type_mean[:], type_block_means[:], axis=mybir.AxisListType.X)
+        minus_block_means = held.tile([P, BLOCKS], F32, name="minus_block_means")
+        minus_type_mean = held.tile([P, 1], F32, name="minus_type_mean")
+        nc.scalar.activation(
+            minus_block_means[:], type_block_means[:], FUNC.Copy, scale=-1.0, accum_out=minus_type_mean[:]
+        )
         type_centred = held.tile([P, BLOCKS], F32, name="type_centred")
-        nc.vector.tensor_scalar(type_centred[:], type_columns, type_mean[:], None, SUBTRACT)
+        nc.scalar.activation(type_centred[:], type_columns, FUNC.Identity, bias=minus_type_mean[:])
 
         gather(0)
         gather(1)

@@ -25,18 +25,18 @@ def tile_gpt_kernel(tc, tok_emb, pos_emb, type_emb, lnf_w, lnf_b, offs, out):
 
         vector_rows = held.tile([P, P], F32, name="vector_rows")
         nc.gpsimd.memset(vector_rows[:], 0.0)
+
+        tok = [held.tile([P, S], F32, name=f"tok{b}") for b in range(BLOCKS)]
+        pos = [[held.tile([P, PIECE], F32, name=f"pos{p}_{b}") for b in range(BLOCKS)] for p in range(PIECES)]
+        for b in range(BLOCKS):
+            nc.sync.dma_start(tok[b][:], tok_emb[b * P : (b + 1) * P, :])
+            nc.scalar.dma_start(pos[0][b][:], pos_emb[b * P : (b + 1) * P, 0:PIECE])
         for k, vector in enumerate((type_emb, lnf_w, lnf_b)):
             nc.scalar.dma_start(
                 vector_rows[k * BLOCKS : (k + 1) * BLOCKS, :], vector.rearrange("(b p) o -> b (p o)", p=P)
             )
-
-        tok = [held.tile([P, S], F32, name=f"tok{b}") for b in range(BLOCKS)]
-        pos = [[held.tile([P, PIECE], F32, name=f"pos{p}_{b}") for b in range(BLOCKS)] for p in range(PIECES)]
-        for p in range(PIECES):
-            for b in range(BLOCKS):
-                if p == 0:
-                    nc.sync.dma_start(tok[b][:], tok_emb[b * P : (b + 1) * P, :])
-                nc.sync.dma_start(pos[p][b][:], pos_emb[b * P : (b + 1) * P, p * PIECE : (p + 1) * PIECE])
+        for b in range(BLOCKS):
+            nc.sync.dma_start(pos[1][b][:], pos_emb[b * P : (b + 1) * P, PIECE : 2 * PIECE])
 
         average = held.tile([P, P], F32, name="average")
         nc.gpsimd.memset(average[:], 1.0 / C)

@@ -9,7 +9,8 @@ P = 128
 C, S, N = 768, 512, 1024
 EPS = 1e-5
 BLOCKS = C // P
-PIECE = 512
+LOAD = 512
+PIECE = 256
 PIECES = N // PIECE
 LIST_COLUMNS = PIECE // 16
 
@@ -19,6 +20,7 @@ def tile_gpt_kernel(tc, tok_emb, pos_emb, type_emb, lnf_w, lnf_b, offs, out):
     with (
         tc.tile_pool(name="held", bufs=1) as held,
         tc.psum_pool(name="psum", bufs=1) as psum,
+        tc.psum_pool(name="sums", bufs=3) as sums,
     ):
         offsets = held.tile([P, N // 16], U16, name="offsets")
         nc.sync.dma_start(offsets[:], offs)
@@ -27,16 +29,16 @@ def tile_gpt_kernel(tc, tok_emb, pos_emb, type_emb, lnf_w, lnf_b, offs, out):
         nc.gpsimd.memset(vector_rows[:], 0.0)
 
         tok = [held.tile([P, S], F32, name=f"tok{b}") for b in range(BLOCKS)]
-        pos = [[held.tile([P, PIECE], F32, name=f"pos{p}_{b}") for b in range(BLOCKS)] for p in range(PIECES)]
+        pos = [[held.tile([P, LOAD], F32, name=f"pos{l}_{b}") for b in range(BLOCKS)] for l in range(N // LOAD)]
         for b in range(BLOCKS):
             nc.sync.dma_start(tok[b][:], tok_emb[b * P : (b + 1) * P, :])
-            nc.scalar.dma_start(pos[0][b][:], pos_emb[b * P : (b + 1) * P, 0:PIECE])
+            nc.scalar.dma_start(pos[0][b][:], pos_emb[b * P : (b + 1) * P, 0:LOAD])
         for k, vector in enumerate((type_emb, lnf_w, lnf_b)):
             nc.scalar.dma_start(
                 vector_rows[k * BLOCKS : (k + 1) * BLOCKS, :], vector.rearrange("(b p) o -> b (p o)", p=P)
             )
         for b in range(BLOCKS):
-            nc.sync.dma_start(pos[1][b][:], pos_emb[b * P : (b + 1) * P, PIECE : 2 * PIECE])
+            nc.sync.dma_start(pos[1][b][:], pos_emb[b * P : (b + 1) * P, LOAD : 2 * LOAD])
 
         average = held.tile([P, P], F32, name="average")
         nc.gpsimd.memset(average[:], 1.0 / C)
@@ -52,19 +54,27 @@ def tile_gpt_kernel(tc, tok_emb, pos_emb, type_emb, lnf_w, lnf_b, offs, out):
         summed = [[held.tile([P, PIECE], F32, name=f"summed{p}_{b}") for b in range(BLOCKS)] for p in range(PIECES)]
         centred = [[held.tile([P, PIECE], F32, name=f"centred{p}_{b}") for b in range(BLOCKS)] for p in range(PIECES)]
         squares = [[held.tile([P, PIECE], BF16, name=f"squares{p}_{b}") for b in range(BLOCKS)] for p in range(PIECES)]
-        mean = [psum.tile([P, PIECE], F32, name=f"mean{p}") for p in range(PIECES)]
-        square_sum = [psum.tile([P, PIECE], F32, name=f"square_sum{p}") for p in range(PIECES)]
+        mean = {}
+        square_sum = {}
         rstd = [held.tile([P, PIECE], F32, name=f"rstd{p}") for p in range(PIECES)]
         normed = [[held.tile([P, PIECE], F32, name=f"normed{p}_{b}") for b in range(BLOCKS)] for p in range(PIECES)]
         result = [[held.tile([P, PIECE], F32, name=f"result{p}_{b}") for b in range(BLOCKS)] for p in range(PIECES)]
 
         def gather(p):
             piece_offsets = offsets[:, p * LIST_COLUMNS : (p + 1) * LIST_COLUMNS]
+            first = (p * PIECE) % LOAD
+            mean[p] = sums.tile([P, PIECE], F32, name="mean")
             for b in range(BLOCKS):
-                nc.vector.tensor_tensor(summed[p][b][:], tok[b][:].indirect(piece_offsets), pos[p][b][:], ADD)
+                nc.vector.tensor_tensor(
+                    summed[p][b][:],
+                    tok[b][:].indirect(piece_offsets),
+                    pos[p * PIECE // LOAD][b][:, first : first + PIECE],
+                    ADD,
+                )
                 nc.tensor.matmul(mean[p][:], average[:], summed[p][b][:], start=(b == 0), stop=(b == BLOCKS - 1))
 
         def centre(p):
+            square_sum[p] = sums.tile([P, PIECE], F32, name="square_sum")
             for b in range(BLOCKS):
                 nc.vector.scalar_tensor_tensor(
                     centred[p][b][:], summed[p][b][:], type_centred[:, b : b + 1], mean[p][:], ADD, SUBTRACT
@@ -108,9 +118,10 @@ def tile_gpt_kernel(tc, tok_emb, pos_emb, type_emb, lnf_w, lnf_b, offs, out):
         type_centred = held.tile([P, BLOCKS], F32, name="type_centred")
         nc.scalar.activation(type_centred[:], type_columns, FUNC.Identity, bias=minus_type_mean[:])
 
-        gather(0)
-        gather(1)
-        centre(0)
-        centre(1)
-        scale(0)
-        scale(1)
+        for step in range(PIECES + 2):
+            if step < PIECES:
+                gather(step)
+            if 0 <= step - 1 < PIECES:
+                centre(step - 1)
+            if 0 <= step - 2:
+                scale(step - 2)

@@ -9,10 +9,10 @@ P = 128
 C, S, N = 768, 512, 1024
 EPS = 1e-5
 BLOCKS = C // P
-LOAD = 512
-PIECE = 256
-PIECES = N // PIECE
-LIST_COLUMNS = PIECE // 16
+WIDTHS = (384, 384, 256)
+PIECES = len(WIDTHS)
+STARTS = tuple(sum(WIDTHS[:p]) for p in range(PIECES))
+assert sum(WIDTHS) == N
 
 
 def tile_gpt_kernel(tc, tok_emb, pos_emb, type_emb, lnf_w, lnf_b, offs, out):
@@ -29,16 +29,17 @@ def tile_gpt_kernel(tc, tok_emb, pos_emb, type_emb, lnf_w, lnf_b, offs, out):
         nc.gpsimd.memset(vector_rows[:], 0.0)
 
         tok = [held.tile([P, S], F32, name=f"tok{b}") for b in range(BLOCKS)]
-        pos = [[held.tile([P, LOAD], F32, name=f"pos{l}_{b}") for b in range(BLOCKS)] for l in range(N // LOAD)]
+        pos = [[held.tile([P, WIDTHS[p]], F32, name=f"pos{p}_{b}") for b in range(BLOCKS)] for p in range(PIECES)]
         for b in range(BLOCKS):
             nc.sync.dma_start(tok[b][:], tok_emb[b * P : (b + 1) * P, :])
-            nc.scalar.dma_start(pos[0][b][:], pos_emb[b * P : (b + 1) * P, 0:LOAD])
+            nc.scalar.dma_start(pos[0][b][:], pos_emb[b * P : (b + 1) * P, 0 : WIDTHS[0]])
         for k, vector in enumerate((type_emb, lnf_w, lnf_b)):
             nc.scalar.dma_start(
                 vector_rows[k * BLOCKS : (k + 1) * BLOCKS, :], vector.rearrange("(b p) o -> b (p o)", p=P)
             )
-        for b in range(BLOCKS):
-            nc.sync.dma_start(pos[1][b][:], pos_emb[b * P : (b + 1) * P, LOAD : 2 * LOAD])
+        for p in range(1, PIECES):
+            for b in range(BLOCKS):
+                nc.sync.dma_start(pos[p][b][:], pos_emb[b * P : (b + 1) * P, STARTS[p] : STARTS[p] + WIDTHS[p]])
 
         average = held.tile([P, P], F32, name="average")
         nc.gpsimd.memset(average[:], 1.0 / C)
@@ -51,30 +52,29 @@ def tile_gpt_kernel(tc, tok_emb, pos_emb, type_emb, lnf_w, lnf_b, offs, out):
         identity = held.tile([P, P], F32, name="identity")
         make_identity(nc, identity[:])
 
-        summed = [[held.tile([P, PIECE], F32, name=f"summed{p}_{b}") for b in range(BLOCKS)] for p in range(PIECES)]
-        centred = [[held.tile([P, PIECE], F32, name=f"centred{p}_{b}") for b in range(BLOCKS)] for p in range(PIECES)]
-        squares = [[held.tile([P, PIECE], BF16, name=f"squares{p}_{b}") for b in range(BLOCKS)] for p in range(PIECES)]
+        summed = [[held.tile([P, WIDTHS[p]], F32, name=f"summed{p}_{b}") for b in range(BLOCKS)] for p in range(PIECES)]
+        centred = [[held.tile([P, WIDTHS[p]], F32, name=f"centred{p}_{b}") for b in range(BLOCKS)] for p in range(PIECES)]
+        squares = [[held.tile([P, WIDTHS[p]], BF16, name=f"squares{p}_{b}") for b in range(BLOCKS)] for p in range(PIECES)]
         mean = {}
         square_sum = {}
-        rstd = [held.tile([P, PIECE], F32, name=f"rstd{p}") for p in range(PIECES)]
-        normed = [[held.tile([P, PIECE], F32, name=f"normed{p}_{b}") for b in range(BLOCKS)] for p in range(PIECES)]
-        result = [[held.tile([P, PIECE], F32, name=f"result{p}_{b}") for b in range(BLOCKS)] for p in range(PIECES)]
+        rstd = [held.tile([P, WIDTHS[p]], F32, name=f"rstd{p}") for p in range(PIECES)]
+        normed = [[held.tile([P, WIDTHS[p]], F32, name=f"normed{p}_{b}") for b in range(BLOCKS)] for p in range(PIECES)]
+        result = [[held.tile([P, WIDTHS[p]], F32, name=f"result{p}_{b}") for b in range(BLOCKS)] for p in range(PIECES)]
 
         def gather(p):
-            piece_offsets = offsets[:, p * LIST_COLUMNS : (p + 1) * LIST_COLUMNS]
-            first = (p * PIECE) % LOAD
-            mean[p] = sums.tile([P, PIECE], F32, name="mean")
+            piece_offsets = offsets[:, STARTS[p] // 16 : (STARTS[p] + WIDTHS[p]) // 16]
+            mean[p] = sums.tile([P, WIDTHS[p]], F32, name="mean")
             for b in range(BLOCKS):
                 nc.vector.tensor_tensor(
                     summed[p][b][:],
                     tok[b][:].indirect(piece_offsets),
-                    pos[p * PIECE // LOAD][b][:, first : first + PIECE],
+                    pos[p][b][:],
                     ADD,
                 )
                 nc.tensor.matmul(mean[p][:], average[:], summed[p][b][:], start=(b == 0), stop=(b == BLOCKS - 1))
 
         def centre(p):
-            square_sum[p] = sums.tile([P, PIECE], F32, name="square_sum")
+            square_sum[p] = sums.tile([P, WIDTHS[p]], F32, name="square_sum")
             for b in range(BLOCKS):
                 nc.vector.scalar_tensor_tensor(
                     centred[p][b][:], summed[p][b][:], type_centred[:, b : b + 1], mean[p][:], ADD, SUBTRACT
@@ -98,7 +98,7 @@ def tile_gpt_kernel(tc, tok_emb, pos_emb, type_emb, lnf_w, lnf_b, offs, out):
                     nc.vector.tensor_scalar(
                         result[p][b][:], normed[p][b][:], lnf_w_columns[:, b : b + 1], lnf_b_columns[:, b : b + 1], MULT, ADD
                     )
-                nc.sync.dma_start(out[b * P : (b + 1) * P, p * PIECE : (p + 1) * PIECE], result[p][b][:])
+                nc.sync.dma_start(out[b * P : (b + 1) * P, STARTS[p] : STARTS[p] + WIDTHS[p]], result[p][b][:])
 
         columns_psum = psum.tile([P, P], F32, name="columns_psum")
         nc.tensor.transpose(columns_psum[:], vector_rows[:], identity[:])

@@ -9,119 +9,199 @@ P = 128
 C, S, N = 768, 512, 1024
 EPS = 1e-5
 BLOCKS = C // P
-WIDTHS = (384, 384, 256)
+WIDTHS = (256, 384, 384)
 PIECES = len(WIDTHS)
 STARTS = tuple(sum(WIDTHS[:p]) for p in range(PIECES))
 assert sum(WIDTHS) == N
+TILES = WIDTHS[0] // P
+LOW = 4
+PARTS = (slice(0, LOW * P), slice(LOW * P, C))
 
 
 def tile_gpt_kernel(tc, tok_emb, pos_emb, type_emb, lnf_w, lnf_b, offs, out):
     nc = tc.nc
     with (
         tc.tile_pool(name="held", bufs=1) as held,
-        tc.psum_pool(name="psum", bufs=1) as psum,
-        tc.psum_pool(name="sums", bufs=3) as sums,
+        tc.psum_pool(name="turned", bufs=2) as turned,
+        tc.psum_pool(name="sums", bufs=2) as sums,
     ):
+        identity = held.tile([P, P], F32, name="identity")
+        make_identity(nc, identity[:])
+
         offsets = held.tile([P, N // 16], U16, name="offsets")
         nc.sync.dma_start(offsets[:], offs)
 
-        vector_rows = held.tile([P, P], F32, name="vector_rows")
-        nc.gpsimd.memset(vector_rows[:], 0.0)
-
         tok = [held.tile([P, S], F32, name=f"tok{b}") for b in range(BLOCKS)]
-        pos = [[held.tile([P, WIDTHS[p]], F32, name=f"pos{p}_{b}") for b in range(BLOCKS)] for p in range(PIECES)]
         for b in range(BLOCKS):
             nc.sync.dma_start(tok[b][:], tok_emb[b * P : (b + 1) * P, :])
-            nc.scalar.dma_start(pos[0][b][:], pos_emb[b * P : (b + 1) * P, 0 : WIDTHS[0]])
-        for k, vector in enumerate((type_emb, lnf_w, lnf_b)):
-            nc.scalar.dma_start(
-                vector_rows[k * BLOCKS : (k + 1) * BLOCKS, :], vector.rearrange("(b p) o -> b (p o)", p=P)
-            )
+        pos_blocks = pos_emb.rearrange("(b p) n -> p b n", p=P)
+        pos0 = [held.tile([P, 2, WIDTHS[0]], F32, name=f"pos0_{h}") for h in range(BLOCKS // 2)]
+        type_columns, lnf_w_columns, lnf_b_columns = (
+            held.tile([P, BLOCKS], F32, name=name) for name in ("type_columns", "lnf_w_columns", "lnf_b_columns")
+        )
+        nc.scalar.dma_start(type_columns[:], type_emb.rearrange("(b p) o -> p (b o)", p=P))
+        for h in range(BLOCKS // 2):
+            nc.scalar.dma_start(pos0[h][:], pos_blocks[:, 2 * h : 2 * h + 2, 0 : WIDTHS[0]])
+        pos = [[held.tile([P, WIDTHS[p]], F32, name=f"pos{p}_{b}") for b in range(BLOCKS)] for p in range(1, PIECES)]
         for p in range(1, PIECES):
             for b in range(BLOCKS):
-                nc.sync.dma_start(pos[p][b][:], pos_emb[b * P : (b + 1) * P, STARTS[p] : STARTS[p] + WIDTHS[p]])
+                nc.sync.dma_start(pos[p - 1][b][:], pos_emb[b * P : (b + 1) * P, STARTS[p] : STARTS[p] + WIDTHS[p]])
+        nc.sync.dma_start(lnf_w_columns[:], lnf_w.rearrange("(b p) o -> p (b o)", p=P))
+        nc.sync.dma_start(lnf_b_columns[:], lnf_b.rearrange("(b p) o -> p (b o)", p=P))
 
-        average = held.tile([P, P], F32, name="average")
-        nc.gpsimd.memset(average[:], 1.0 / C)
-        ones = held.tile([P, P], BF16, name="ones")
-        nc.gpsimd.memset(ones[:], 1.0)
         eps = held.tile([P, 1], F32, name="eps")
         nc.gpsimd.memset(eps[:], EPS)
         warm = held.tile([P, 1], F32, name="warm")
         nc.scalar.activation(warm[:], eps[:], FUNC.Abs_reciprocal_sqrt)
-        identity = held.tile([P, P], F32, name="identity")
-        make_identity(nc, identity[:])
+        zeros = held.tile([P, P], F32, name="zeros")
+        nc.gpsimd.memset(zeros[:], 0.0)
+        average = held.tile([P, P], F32, name="average")
+        nc.gpsimd.memset(average[:], 1.0 / C)
+        ones = held.tile([P, P], BF16, name="ones")
+        nc.gpsimd.memset(ones[:], 1.0)
 
-        summed = [[held.tile([P, WIDTHS[p]], F32, name=f"summed{p}_{b}") for b in range(BLOCKS)] for p in range(PIECES)]
-        centred = [[held.tile([P, WIDTHS[p]], F32, name=f"centred{p}_{b}") for b in range(BLOCKS)] for p in range(PIECES)]
-        squares = [[held.tile([P, WIDTHS[p]], BF16, name=f"squares{p}_{b}") for b in range(BLOCKS)] for p in range(PIECES)]
-        mean = {}
-        square_sum = {}
-        rstd = [held.tile([P, WIDTHS[p]], F32, name=f"rstd{p}") for p in range(PIECES)]
-        normed = [[held.tile([P, WIDTHS[p]], F32, name=f"normed{p}_{b}") for b in range(BLOCKS)] for p in range(PIECES)]
-        result = [[held.tile([P, WIDTHS[p]], F32, name=f"result{p}_{b}") for b in range(BLOCKS)] for p in range(PIECES)]
-
-        def gather(p):
-            piece_offsets = offsets[:, STARTS[p] // 16 : (STARTS[p] + WIDTHS[p]) // 16]
-            mean[p] = sums.tile([P, WIDTHS[p]], F32, name="mean")
-            for b in range(BLOCKS):
-                nc.vector.tensor_tensor(
-                    summed[p][b][:],
-                    tok[b][:].indirect(piece_offsets),
-                    pos[p][b][:],
-                    ADD,
-                )
-                nc.tensor.matmul(mean[p][:], average[:], summed[p][b][:], start=(b == 0), stop=(b == BLOCKS - 1))
-
-        def centre(p):
-            square_sum[p] = sums.tile([P, WIDTHS[p]], F32, name="square_sum")
-            for b in range(BLOCKS):
-                nc.vector.scalar_tensor_tensor(
-                    centred[p][b][:], summed[p][b][:], type_centred[:, b : b + 1], mean[p][:], ADD, SUBTRACT
-                )
-                nc.scalar.activation(squares[p][b][:], centred[p][b][:], FUNC.Square)
-                nc.tensor.matmul(square_sum[p][:], ones[:], squares[p][b][:], start=(b == 0), stop=(b == BLOCKS - 1))
-            nc.scalar.activation(rstd[p][:], square_sum[p][:], FUNC.Abs_reciprocal_sqrt, bias=eps[:], scale=1.0 / C)
-
-        def scale(p):
-            for b in range(BLOCKS):
-                nc.vector.tensor_tensor(normed[p][b][:], centred[p][b][:], rstd[p][:], MULT)
-                if b < BLOCKS - 1:
-                    nc.scalar.activation(
-                        result[p][b][:],
-                        normed[p][b][:],
-                        FUNC.Identity,
-                        bias=lnf_b_columns[:, b : b + 1],
-                        scale=lnf_w_columns[:, b : b + 1],
-                    )
-                else:
-                    nc.vector.tensor_scalar(
-                        result[p][b][:], normed[p][b][:], lnf_w_columns[:, b : b + 1], lnf_b_columns[:, b : b + 1], MULT, ADD
-                    )
-                nc.sync.dma_start(out[b * P : (b + 1) * P, STARTS[p] : STARTS[p] + WIDTHS[p]], result[p][b][:])
-
-        columns_psum = psum.tile([P, P], F32, name="columns_psum")
-        nc.tensor.transpose(columns_psum[:], vector_rows[:], identity[:])
-        columns = held.tile([P, 3 * BLOCKS], F32, name="columns")
-        nc.scalar.copy(columns[:], columns_psum[:, 0 : 3 * BLOCKS])
-        type_columns = columns[:, 0:BLOCKS]
-        lnf_w_columns = columns[:, BLOCKS : 2 * BLOCKS]
-        lnf_b_columns = columns[:, 2 * BLOCKS : 3 * BLOCKS]
-
-        type_block_means = psum.tile([P, BLOCKS], F32, name="type_block_means")
-        nc.tensor.matmul(type_block_means[:], average[:], type_columns, start=True, stop=True)
+        type_wide = [held.tile([P, P], F32, name=f"type_wide{b}") for b in range(BLOCKS)]
+        for b in range(BLOCKS):
+            nc.scalar.activation(type_wide[b][:], zeros[:], FUNC.Identity, bias=type_columns[:, b : b + 1])
+        type_block_means = sums.tile([P, BLOCKS], F32, name="type_block_means", tag="square_sum")
+        nc.tensor.matmul(type_block_means[:], average[:], type_columns[:], start=True, stop=True)
         minus_block_means = held.tile([P, BLOCKS], F32, name="minus_block_means")
         minus_type_mean = held.tile([P, 1], F32, name="minus_type_mean")
         nc.scalar.activation(
             minus_block_means[:], type_block_means[:], FUNC.Copy, scale=-1.0, accum_out=minus_type_mean[:]
         )
         type_centred = held.tile([P, BLOCKS], F32, name="type_centred")
-        nc.scalar.activation(type_centred[:], type_columns, FUNC.Identity, bias=minus_type_mean[:])
+        nc.scalar.activation(type_centred[:], type_columns[:], FUNC.Identity, bias=minus_type_mean[:])
 
-        for step in range(PIECES + 2):
-            if step < PIECES:
-                gather(step)
-            if 0 <= step - 1 < PIECES:
-                centre(step - 1)
-            if 0 <= step - 2:
-                scale(step - 2)
+        summed = [[held.tile([P, WIDTHS[p]], F32, name=f"summed{p}_{b}") for b in range(BLOCKS)] for p in range(PIECES)]
+        result = [[held.tile([P, WIDTHS[p]], F32, name=f"result{p}_{b}") for b in range(BLOCKS)] for p in range(PIECES)]
+
+        def gather(p):
+            piece_offsets = offsets[:, STARTS[p] // 16 : (STARTS[p] + WIDTHS[p]) // 16]
+            for b in range(BLOCKS):
+                pos_block = pos0[b // 2][:, b % 2, :] if p == 0 else pos[p - 1][b][:]
+                nc.vector.tensor_tensor(summed[p][b][:], tok[b][:].indirect(piece_offsets), pos_block, ADD)
+
+        def store(p, b):
+            nc.sync.dma_start(out[b * P : (b + 1) * P, STARTS[p] : STARTS[p] + WIDTHS[p]], result[p][b][:])
+
+        turned_tile = {}
+        minus_mean = held.tile([P, TILES], F32, name="minus_mean")
+        minus_mean_part = [held.tile([P, TILES], F32, name=f"minus_mean_part{k}") for k in range(2)]
+        square_sum0 = [held.tile([P, TILES], F32, name=f"square_sum0_{k}") for k in range(2)]
+        second_part = held.tile([P, TILES], F32, name="second_part")
+        rstd0 = held.tile([P, TILES], F32, name="rstd0")
+        shift = held.tile([P, TILES], F32, name="shift")
+        normed0 = [held.tile([P, C], F32, name=f"normed0_{t}", tag=f"centred1_{t}") for t in range(TILES)]
+
+        def tokens_of(t, b):
+            return summed[0][b][:, t * P : (t + 1) * P]
+
+        def turn(t):
+            turned_tile[t] = [turned.tile([P, LOW * P], F32, name=name) for name in ("low", "high")]
+            for b in range(BLOCKS):
+                block = turned_tile[t][b // LOW][:, (b % LOW) * P : (b % LOW + 1) * P]
+                nc.tensor.matmul(block, type_wide[b][:], identity[:], start=True, stop=False, is_transpose=True)
+                nc.tensor.matmul(block, tokens_of(t, b), identity[:], start=False, stop=True, is_transpose=True)
+
+        def parts(t):
+            return [(turned_tile[t][k][:, 0 : part.stop - part.start], part) for k, part in enumerate(PARTS)]
+
+        def normalise_turned():
+            for t in range(TILES):
+                column = slice(t, t + 1)
+                for k, (bank, part) in enumerate(parts(t)):
+                    minus_parts0 = held.tile([P, part.stop - part.start], BF16, name=f"minus_parts0_{t}_{k}")
+                    nc.scalar.activation(
+                        minus_parts0[:], bank, FUNC.Copy, scale=-1.0 / C, accum_out=minus_mean_part[k][:, column]
+                    )
+                nc.scalar.activation(
+                    minus_mean[:, column],
+                    minus_mean_part[0][:, column],
+                    FUNC.Identity,
+                    bias=minus_mean_part[1][:, column],
+                )
+                for k, (bank, part) in enumerate(parts(t)):
+                    squares0 = held.tile([P, part.stop - part.start], BF16, name=f"squares0_{t}_{k}")
+                    nc.scalar.activation(
+                        squares0[:], bank, FUNC.Square, bias=minus_mean[:, column], accum_out=square_sum0[k][:, column]
+                    )
+            nc.scalar.activation(second_part[:], square_sum0[1][:], FUNC.Identity, bias=eps[:], scale=1.0 / C)
+            for t in range(TILES):
+                column = slice(t, t + 1)
+                nc.scalar.activation(
+                    rstd0[:, column],
+                    square_sum0[0][:, column],
+                    FUNC.Abs_reciprocal_sqrt,
+                    bias=second_part[:, column],
+                    scale=1.0 / C,
+                )
+                nc.scalar.activation(shift[:, column], minus_mean[:, column], FUNC.Copy, scale=rstd0[:, column])
+                for bank, part in parts(t):
+                    nc.scalar.activation(
+                        normed0[t][:, part], bank, FUNC.Identity, bias=shift[:, column], scale=rstd0[:, column]
+                    )
+
+        def finish_turned():
+            for first in range(0, BLOCKS, 2):
+                tag = "low" if first < LOW else "high"
+                turned_back = turned.tile([P, 2, WIDTHS[0]], F32, name="turned_back", tag=tag)
+                for b in (first, first + 1):
+                    for t in range(TILES):
+                        nc.tensor.transpose(
+                            turned_back[:, b - first, t * P : (t + 1) * P], normed0[t][:, b * P : (b + 1) * P], identity[:]
+                        )
+                for b in (first, first + 1):
+                    nc.scalar.activation(
+                        result[0][b][:],
+                        turned_back[:, b - first, :],
+                        FUNC.Identity,
+                        bias=lnf_b_columns[:, b : b + 1],
+                        scale=lnf_w_columns[:, b : b + 1],
+                    )
+                    store(0, b)
+
+        centred = [[held.tile([P, WIDTHS[p]], F32, name=f"centred{p}_{b}") for b in range(BLOCKS)] for p in range(1, PIECES)]
+        normed = [[held.tile([P, WIDTHS[p]], F32, name=f"normed{p}_{b}") for b in range(BLOCKS)] for p in range(1, PIECES)]
+        squares = [[held.tile([P, WIDTHS[p]], BF16, name=f"squares{p}_{b}") for b in range(BLOCKS)] for p in range(1, PIECES)]
+        rstd = [held.tile([P, WIDTHS[p]], F32, name=f"rstd{p}") for p in range(1, PIECES)]
+        mean = {}
+
+        def average_channels(p):
+            mean[p] = sums.tile([P, WIDTHS[p]], F32, name="mean")
+            for b in range(BLOCKS):
+                nc.tensor.matmul(mean[p][:], average[:], summed[p][b][:], start=(b == 0), stop=(b == BLOCKS - 1))
+
+        def centre(p):
+            square_sum = sums.tile([P, WIDTHS[p]], F32, name="square_sum")
+            for b in range(BLOCKS):
+                nc.vector.scalar_tensor_tensor(
+                    centred[p - 1][b][:], summed[p][b][:], type_centred[:, b : b + 1], mean[p][:], ADD, SUBTRACT
+                )
+                nc.scalar.activation(squares[p - 1][b][:], centred[p - 1][b][:], FUNC.Square)
+                nc.tensor.matmul(square_sum[:], ones[:], squares[p - 1][b][:], start=(b == 0), stop=(b == BLOCKS - 1))
+            nc.scalar.activation(rstd[p - 1][:], square_sum[:], FUNC.Abs_reciprocal_sqrt, bias=eps[:], scale=1.0 / C)
+
+        def scale(p):
+            for b in range(BLOCKS):
+                w, shift_b = lnf_w_columns[:, b : b + 1], lnf_b_columns[:, b : b + 1]
+                nc.vector.tensor_tensor(normed[p - 1][b][:], centred[p - 1][b][:], rstd[p - 1][:], MULT)
+                if b < BLOCKS - 1:
+                    nc.scalar.activation(result[p][b][:], normed[p - 1][b][:], FUNC.Identity, bias=shift_b, scale=w)
+                else:
+                    nc.vector.tensor_scalar(result[p][b][:], normed[p - 1][b][:], w, shift_b, MULT, ADD)
+                store(p, b)
+
+        gather(0)
+        for t in range(TILES):
+            turn(t)
+        normalise_turned()
+        gather(1)
+        average_channels(1)
+        finish_turned()
+        gather(2)
+        average_channels(2)
+        centre(1)
+        centre(2)
+        scale(1)
+        scale(2)

import concourse.mybir as mybir
from concourse.masks import make_identity

F32, BF16, U16 = mybir.dt.float32, mybir.dt.bfloat16, mybir.dt.uint16
ADD, SUBTRACT, MULT = mybir.AluOpType.add, mybir.AluOpType.subtract, mybir.AluOpType.mult
FUNC = mybir.ActivationFunctionType

P = 128
C, S, N = 768, 512, 1024
EPS = 1e-5
BLOCKS = C // P
WIDTHS = (256, 384, 384)
PIECES = len(WIDTHS)
STARTS = tuple(sum(WIDTHS[:p]) for p in range(PIECES))
assert sum(WIDTHS) == N
TILES = WIDTHS[0] // P
LOW = 4
PARTS = (slice(0, LOW * P), slice(LOW * P, C))


def tile_gpt_kernel(tc, tok_emb, pos_emb, type_emb, lnf_w, lnf_b, offs, out):
    nc = tc.nc
    with (
        tc.tile_pool(name="held", bufs=1) as held,
        tc.psum_pool(name="turned", bufs=2) as turned,
        tc.psum_pool(name="sums", bufs=2) as sums,
    ):
        identity = held.tile([P, P], F32, name="identity")
        make_identity(nc, identity[:])

        offsets = held.tile([P, N // 16], U16, name="offsets")
        nc.sync.dma_start(offsets[:], offs)

        tok = [held.tile([P, S], F32, name=f"tok{b}") for b in range(BLOCKS)]
        for b in range(BLOCKS):
            nc.sync.dma_start(tok[b][:], tok_emb[b * P : (b + 1) * P, :])
        pos_blocks = pos_emb.rearrange("(b p) n -> p b n", p=P)
        pos0 = [held.tile([P, 2, WIDTHS[0]], F32, name=f"pos0_{h}") for h in range(BLOCKS // 2)]
        type_columns, lnf_w_columns, lnf_b_columns = (
            held.tile([P, BLOCKS], F32, name=name) for name in ("type_columns", "lnf_w_columns", "lnf_b_columns")
        )
        nc.scalar.dma_start(type_columns[:], type_emb.rearrange("(b p) o -> p (b o)", p=P))
        for h in range(BLOCKS // 2):
            nc.scalar.dma_start(pos0[h][:], pos_blocks[:, 2 * h : 2 * h + 2, 0 : WIDTHS[0]])
        pos = [[held.tile([P, WIDTHS[p]], F32, name=f"pos{p}_{b}") for b in range(BLOCKS)] for p in range(1, PIECES)]
        for p in range(1, PIECES):
            for b in range(BLOCKS):
                nc.sync.dma_start(pos[p - 1][b][:], pos_emb[b * P : (b + 1) * P, STARTS[p] : STARTS[p] + WIDTHS[p]])
        nc.sync.dma_start(lnf_w_columns[:], lnf_w.rearrange("(b p) o -> p (b o)", p=P))
        nc.sync.dma_start(lnf_b_columns[:], lnf_b.rearrange("(b p) o -> p (b o)", p=P))

        eps = held.tile([P, 1], F32, name="eps")
        nc.gpsimd.memset(eps[:], EPS)
        warm = held.tile([P, 1], F32, name="warm")
        nc.scalar.activation(warm[:], eps[:], FUNC.Abs_reciprocal_sqrt)
        zeros = held.tile([P, P], F32, name="zeros")
        nc.gpsimd.memset(zeros[:], 0.0)
        average = held.tile([P, P], F32, name="average")
        nc.gpsimd.memset(average[:], 1.0 / C)
        ones = held.tile([P, P], BF16, name="ones")
        nc.gpsimd.memset(ones[:], 1.0)

        type_wide = [held.tile([P, P], F32, name=f"type_wide{b}") for b in range(BLOCKS)]
        for b in range(BLOCKS):
            nc.scalar.activation(type_wide[b][:], zeros[:], FUNC.Identity, bias=type_columns[:, b : b + 1])
        type_block_means = sums.tile([P, BLOCKS], F32, name="type_block_means", tag="square_sum")
        nc.tensor.matmul(type_block_means[:], average[:], type_columns[:], start=True, stop=True)
        minus_block_means = held.tile([P, BLOCKS], F32, name="minus_block_means")
        minus_type_mean = held.tile([P, 1], F32, name="minus_type_mean")
        nc.scalar.activation(
            minus_block_means[:], type_block_means[:], FUNC.Copy, scale=-1.0, accum_out=minus_type_mean[:]
        )
        type_centred = held.tile([P, BLOCKS], F32, name="type_centred")
        nc.scalar.activation(type_centred[:], type_columns[:], FUNC.Identity, bias=minus_type_mean[:])

        summed = [[held.tile([P, WIDTHS[p]], F32, name=f"summed{p}_{b}") for b in range(BLOCKS)] for p in range(PIECES)]
        result = [[held.tile([P, WIDTHS[p]], F32, name=f"result{p}_{b}") for b in range(BLOCKS)] for p in range(PIECES)]

        def gather(p):
            piece_offsets = offsets[:, STARTS[p] // 16 : (STARTS[p] + WIDTHS[p]) // 16]
            for b in range(BLOCKS):
                pos_block = pos0[b // 2][:, b % 2, :] if p == 0 else pos[p - 1][b][:]
                nc.vector.tensor_tensor(summed[p][b][:], tok[b][:].indirect(piece_offsets), pos_block, ADD)

        def store(p, b):
            nc.sync.dma_start(out[b * P : (b + 1) * P, STARTS[p] : STARTS[p] + WIDTHS[p]], result[p][b][:])

        turned_tile = {}
        minus_mean = held.tile([P, TILES], F32, name="minus_mean")
        minus_mean_part = [held.tile([P, TILES], F32, name=f"minus_mean_part{k}") for k in range(2)]
        square_sum0 = [held.tile([P, TILES], F32, name=f"square_sum0_{k}") for k in range(2)]
        second_part = held.tile([P, TILES], F32, name="second_part")
        rstd0 = held.tile([P, TILES], F32, name="rstd0")
        shift = held.tile([P, TILES], F32, name="shift")
        normed0 = [held.tile([P, C], F32, name=f"normed0_{t}", tag=f"centred1_{t}") for t in range(TILES)]

        def tokens_of(t, b):
            return summed[0][b][:, t * P : (t + 1) * P]

        def turn(t):
            turned_tile[t] = [turned.tile([P, LOW * P], F32, name=name) for name in ("low", "high")]
            for b in range(BLOCKS):
                block = turned_tile[t][b // LOW][:, (b % LOW) * P : (b % LOW + 1) * P]
                nc.tensor.matmul(block, type_wide[b][:], identity[:], start=True, stop=False, is_transpose=True)
                nc.tensor.matmul(block, tokens_of(t, b), identity[:], start=False, stop=True, is_transpose=True)

        def parts(t):
            return [(turned_tile[t][k][:, 0 : part.stop - part.start], part) for k, part in enumerate(PARTS)]

        def normalise_turned():
            for t in range(TILES):
                column = slice(t, t + 1)
                for k, (bank, part) in enumerate(parts(t)):
                    minus_parts0 = held.tile([P, part.stop - part.start], BF16, name=f"minus_parts0_{t}_{k}")
                    nc.scalar.activation(
                        minus_parts0[:], bank, FUNC.Copy, scale=-1.0 / C, accum_out=minus_mean_part[k][:, column]
                    )
                nc.scalar.activation(
                    minus_mean[:, column],
                    minus_mean_part[0][:, column],
                    FUNC.Identity,
                    bias=minus_mean_part[1][:, column],
                )
                for k, (bank, part) in enumerate(parts(t)):
                    squares0 = held.tile([P, part.stop - part.start], BF16, name=f"squares0_{t}_{k}")
                    nc.scalar.activation(
                        squares0[:], bank, FUNC.Square, bias=minus_mean[:, column], accum_out=square_sum0[k][:, column]
                    )
            nc.scalar.activation(second_part[:], square_sum0[1][:], FUNC.Identity, bias=eps[:], scale=1.0 / C)
            for t in range(TILES):
                column = slice(t, t + 1)
                nc.scalar.activation(
                    rstd0[:, column],
                    square_sum0[0][:, column],
                    FUNC.Abs_reciprocal_sqrt,
                    bias=second_part[:, column],
                    scale=1.0 / C,
                )
                nc.scalar.activation(shift[:, column], minus_mean[:, column], FUNC.Copy, scale=rstd0[:, column])
                for bank, part in parts(t):
                    nc.scalar.activation(
                        normed0[t][:, part], bank, FUNC.Identity, bias=shift[:, column], scale=rstd0[:, column]
                    )

        def finish_turned():
            for first in range(0, BLOCKS, 2):
                tag = "low" if first < LOW else "high"
                turned_back = turned.tile([P, 2, WIDTHS[0]], F32, name="turned_back", tag=tag)
                for b in (first, first + 1):
                    for t in range(TILES):
                        nc.tensor.transpose(
                            turned_back[:, b - first, t * P : (t + 1) * P], normed0[t][:, b * P : (b + 1) * P], identity[:]
                        )
                for b in (first, first + 1):
                    nc.scalar.activation(
                        result[0][b][:],
                        turned_back[:, b - first, :],
                        FUNC.Identity,
                        bias=lnf_b_columns[:, b : b + 1],
                        scale=lnf_w_columns[:, b : b + 1],
                    )
                    store(0, b)

        centred = [[held.tile([P, WIDTHS[p]], F32, name=f"centred{p}_{b}") for b in range(BLOCKS)] for p in range(1, PIECES)]
        normed = [[held.tile([P, WIDTHS[p]], F32, name=f"normed{p}_{b}") for b in range(BLOCKS)] for p in range(1, PIECES)]
        squares = [[held.tile([P, WIDTHS[p]], BF16, name=f"squares{p}_{b}") for b in range(BLOCKS)] for p in range(1, PIECES)]
        rstd = [held.tile([P, WIDTHS[p]], F32, name=f"rstd{p}") for p in range(1, PIECES)]
        mean = {}

        def average_channels(p):
            mean[p] = sums.tile([P, WIDTHS[p]], F32, name="mean")
            for b in range(BLOCKS):
                nc.tensor.matmul(mean[p][:], average[:], summed[p][b][:], start=(b == 0), stop=(b == BLOCKS - 1))

        def centre(p):
            square_sum = sums.tile([P, WIDTHS[p]], F32, name="square_sum")
            for b in range(BLOCKS):
                nc.vector.scalar_tensor_tensor(
                    centred[p - 1][b][:], summed[p][b][:], type_centred[:, b : b + 1], mean[p][:], ADD, SUBTRACT
                )
                nc.scalar.activation(squares[p - 1][b][:], centred[p - 1][b][:], FUNC.Square)
                nc.tensor.matmul(square_sum[:], ones[:], squares[p - 1][b][:], start=(b == 0), stop=(b == BLOCKS - 1))
            nc.scalar.activation(rstd[p - 1][:], square_sum[:], FUNC.Abs_reciprocal_sqrt, bias=eps[:], scale=1.0 / C)

        def scale(p):
            for b in range(BLOCKS):
                w, shift_b = lnf_w_columns[:, b : b + 1], lnf_b_columns[:, b : b + 1]
                nc.vector.tensor_tensor(normed[p - 1][b][:], centred[p - 1][b][:], rstd[p - 1][:], MULT)
                if b < BLOCKS - 1:
                    nc.scalar.activation(result[p][b][:], normed[p - 1][b][:], FUNC.Identity, bias=shift_b, scale=w)
                else:
                    nc.vector.tensor_scalar(result[p][b][:], normed[p - 1][b][:], w, shift_b, MULT, ADD)
                store(p, b)

        gather(0)
        for t in range(TILES):
            turn(t)
        normalise_turned()
        gather(1)
        average_channels(1)
        finish_turned()
        gather(2)
        average_channels(2)
        centre(1)
        centre(2)
        scale(1)
        scale(2)
